import numpy as np
import ml_dtypes


def mxq(x, axis, fmt="e4m3"):
    dtype, down = {"e4m3": (ml_dtypes.float8_e4m3fn, 7), "e5m2": (ml_dtypes.float8_e5m2, 14)}[fmt]
    v = np.moveaxis(np.asarray(x, np.float32).astype(ml_dtypes.bfloat16).astype(np.float64), axis, -1)
    blocks = v.reshape(v.shape[:-1] + (-1, 32))
    amax = np.abs(blocks).max(-1, keepdims=True)
    byte = np.maximum(np.where(amax > 0, np.frexp(amax)[1] - 1 + 127, 0) - down, 1)
    scale = np.exp2(byte - 127.0)
    codes = (blocks / scale).astype(np.float32).astype(dtype).astype(np.float64)
    return np.moveaxis((codes * scale).reshape(v.shape), -1, axis)


WIDE = False


def mx_kscale(k):
    if not WIDE:
        return np.ones(k)
    levels = np.array([10, -10, 5, -5, 0])
    a = np.random.permutation(np.resize(levels, k // 512 * 4)).reshape(k // 512, 4)
    idx = np.arange(k)
    return np.exp2(a[idx // 512, idx % 128 // 32])


BF16 = ml_dtypes.bfloat16


def bf(x):
    return np.asarray(x, np.float32).astype(BF16)


def f64(x):
    return np.asarray(x).astype(np.float64)


E2M1 = np.array([0.0, 0.5, 1.0, 1.5, 2.0, 3.0, 4.0, 6.0, -0.0, -0.5, -1.0, -1.5, -2.0, -3.0, -4.0, -6.0])


def pack_weight(w, fmt):
    k, n = w.shape
    w = f64(bf(w)).reshape(k // 32, 32, n)
    amax = np.abs(w).max(1)
    if fmt == "e4m3":
        byte = np.frexp(amax)[1] - 1 + 127 - 7
    else:
        mant, ex = np.frexp(amax / 6.0)
        byte = np.where(mant > 0.5, ex, ex - 1) + 127
    byte = np.clip(np.where(amax > 0, byte, 1), 1, 254)
    scaled = (w * np.exp2(127.0 - byte)[:, None, :]).reshape(k, n).astype(np.float32)
    by_word = np.ascontiguousarray(scaled.reshape(k // 512, 128, 4, n).transpose(0, 1, 3, 2))
    if fmt == "e4m3":
        words = by_word.astype(ml_dtypes.float8_e4m3fn).view(np.uint8)
    else:
        c = by_word.astype(ml_dtypes.float4_e2m1fn).view(np.uint8) & 0xF
        words = c[..., 0::2] | (c[..., 1::2] << 4)
    return np.ascontiguousarray(words), np.ascontiguousarray(byte.astype(np.uint8).reshape(k // 512, 16, n))


def unpack_weight(words, scales, fmt):
    g, p, n, _ = words.shape
    if fmt == "e4m3":
        vals = np.ascontiguousarray(words).view(ml_dtypes.float8_e4m3fn).astype(np.float64)
    else:
        nib = np.empty((g, p, n, 4), np.uint8)
        nib[..., 0::2] = words & 0xF
        nib[..., 1::2] = words >> 4
        vals = E2M1[nib]
    vals = vals * np.repeat(np.exp2(scales.astype(np.float64) - 127.0), 8, axis=1)[..., None]
    return vals.transpose(0, 1, 3, 2).reshape(g * 512, n)

def pack4(w):
    words, scales = pack_weight(w, "e2m1")
    return words.reshape(words.shape[0], 128, -1), scales


def unpack4(words, scales):
    return unpack_weight(words.reshape(words.shape[0], 128, -1, 2), scales, "e2m1")


B, T, HS, C, NH, HD, WS, MAXD = 2, 8, 28, 512, 8, 16, 7, 3
N = T * HS * HS
E = NH * HD
BT = B * NH * T
EPS = 1e-12


def l2norm(v, axis):
    return v / np.maximum(np.sqrt(np.sum(v * v, axis=axis, keepdims=True)), EPS)


def setup_inputs():
    s = mx_kscale(C)
    x = bf(np.random.standard_normal((B, N, C)) * s)
    q_w_words, q_w_scales = pack4((np.random.standard_normal((E, C)) / np.sqrt(C) / s).T)
    k_w_words, k_w_scales = pack4((np.random.standard_normal((E, C)) / np.sqrt(C) / s).T)
    return {"x": x,
            "q_w_words": q_w_words, "q_w_scales": q_w_scales,
            "k_w_words": k_w_words, "k_w_scales": k_w_scales}


def reference(x, q_w_words, q_w_scales, k_w_words, k_w_scales):
    xq = mxq(f64(x), 2, "e4m3")
    q = xq @ unpack4(q_w_words, q_w_scales)
    k = xq @ unpack4(k_w_words, k_w_scales)
    q = q.reshape(B, N, NH, HD).transpose(0, 2, 1, 3)
    k = k.reshape(B, N, NH, HD).transpose(0, 2, 1, 3)
    q = q.reshape(B * NH, T, HS, HS, HD).transpose(0, 1, 4, 2, 3)
    k = k.reshape(B * NH, T, HS, HS, HD).transpose(0, 1, 4, 2, 3)
    k_post = np.concatenate([k[:, 1:], k[:, -1:]], axis=1)
    qp = l2norm(q.reshape(BT, HD, HS, HS), 1)
    kp = l2norm(k_post.reshape(BT, HD, HS, HS), 1)
    return qp, kp

@@ -1,0 +1,239 @@
+from contextlib import ExitStack
+
+import concourse.mybir as mybir
+from concourse.masks import make_identity
+
+F32 = mybir.dt.float32
+BF16 = mybir.dt.bfloat16
+I32 = mybir.dt.int32
+U32 = mybir.dt.uint32
+U8 = mybir.dt.uint8
+FP8X4 = mybir.dt.float8_e4m3fn_x4
+FP4X4 = mybir.dt.float4_e2m1fn_x4
+ACT = mybir.ActivationFunctionType
+ALU = mybir.AluOpType
+AXIS = mybir.AxisListType
+
+P = 128
+CLIPS = 2
+FRAMES = 8
+FRAME_TOKENS = 28 * 28
+CHANNELS = 512
+HEADS = 8
+HEAD_DIM = 16
+TOKENS = CLIPS * FRAMES * FRAME_TOKENS
+PAIR_TOKENS = 2 * P
+PAIRS = TOKENS // PAIR_TOKENS
+GROUPS = 2 * 2 * HEADS
+TINY = 1e-24
+
+LOADS_AHEAD = 8
+LAST_LAG = 4
+
+FLOPS = 2 * TOKENS * CHANNELS * 2 * HEADS * HEAD_DIM
+
+
+def tile_costvolumeattention17_pa_t_kernel(
+    tc, x, q_w_words, q_w_scales, k_w_words, k_w_scales, out_0, out_1
+):
+    nc = tc.nc
+    x_pairs = x.rearrange("b n c -> (b n) c").rearrange("(u p j) c -> u p (j c)", p=P, j=2)
+    q_rows = out_0.rearrange("(b h t) d i j -> b t d h (i j)", b=CLIPS, h=HEADS)
+    k_rows = out_1.rearrange("(b h t) d i j -> b t d h (i j)", b=CLIPS, h=HEADS)
+
+    with ExitStack() as ctx:
+        const = ctx.enter_context(tc.tile_pool(name="const", bufs=1))
+        x_pool = ctx.enter_context(tc.tile_pool(name="x", bufs=LOADS_AHEAD + 1))
+        work = ctx.enter_context(tc.tile_pool(name="work", bufs=3))
+        stage_pool = ctx.enter_context(tc.tile_pool(name="stage", bufs=4))
+        xt_pool = ctx.enter_context(tc.psum_pool(name="xt", bufs=2))
+        qk_pool = ctx.enter_context(tc.psum_pool(name="qk", bufs=3))
+        ot_pool = ctx.enter_context(tc.psum_pool(name="ot", bufs=3))
+        ctx.enter_context(tc.manual_schedule())
+
+        x_tiles = {}
+        xt_tiles = {}
+        grouped_tiles = {}
+        code_tiles = {}
+        plane_tiles = {}
+        qk_tiles = {}
+        square_tiles = {}
+        norm_tiles = {}
+        unit_tiles = {}
+        ot_tiles = {}
+        stage_tiles = {}
+
+        def load(u):
+            x_sb = x_pool.tile([P, 2 * CHANNELS], BF16)
+            nc.sync.dma_start(out=x_sb[:], in_=x_pairs[u])
+            x_tiles[u] = x_sb
+
+        load(0)
+        w_words = const.tile([P, 2 * 2 * P], U8, align_bytes=64)
+        w_planes = const.tile([P, 2 * P], U8, align_bytes=64)
+        nc.vector.memset(w_planes[:].bitcast(I32), 0)
+        for c, (words, scales) in enumerate(((q_w_words, q_w_scales), (k_w_words, k_w_scales))):
+            nc.sync.dma_start(
+                out=w_words[:, 2 * P * c : 2 * P * (c + 1)].bitcast(I32), in_=words[0].bitcast(I32)
+            )
+            for quad in range(4):
+                nc.sync.dma_start(
+                    out=w_planes[32 * quad : 32 * quad + 4, P * c : P * (c + 1)].bitcast(I32),
+                    in_=scales[0, 4 * quad : 4 * quad + 4, :].bitcast(I32),
+                )
+        for u in range(1, LOADS_AHEAD):
+            load(u)
+        ident = const.tile([P, P], F32)
+        make_identity(nc, ident[:])
+        warm = const.tile([P, 1], F32)
+        nc.vector.memset(warm[:], 1.0)
+        nc.scalar.sqrt(out=warm[:], in_=warm[:])
+
+        def transpose_x(u):
+            words = x_tiles[u][:].bitcast(F32)
+            xt = xt_pool.tile([P, 2, 2, P], F32)
+            for j in range(2):
+                for half in range(2):
+                    first = (CHANNELS // 2) * j + half
+                    nc.tensor.transpose(
+                        xt[:, j, half, :], words[:, first : (CHANNELS // 2) * (j + 1) : 2], ident[:]
+                    )
+            xt_tiles[u] = xt
+
+        def group_x(u):
+            grouped = work.tile([P, 2, P, 4], BF16, align_bytes=64)
+            nc.scalar.copy(
+                out=grouped[:]
+                .rearrange("p j n t -> p (j n t)")
+                .bitcast(F32)
+                .rearrange("p (j n half) -> p j n half", j=2, half=2),
+                in_=xt_tiles[u][:].rearrange("p j half n -> p j n half"),
+            )
+            grouped_tiles[u] = grouped
+
+        def quantise_x(u):
+            codes = work.tile([P, PAIR_TOKENS], U32, align_bytes=64)
+            planes = work.tile([P, PAIR_TOKENS], U8, align_bytes=64)
+            nc.vector.quantize_mx(
+                out=codes[:].bitcast(FP8X4),
+                scales=planes[:],
+                in_=grouped_tiles[u][:].rearrange("p j n t -> p (j n t)"),
+            )
+            code_tiles[u] = codes
+            plane_tiles[u] = planes
+
+        def project(u):
+            codes = code_tiles[u]
+            planes = plane_tiles[u]
+            qk = qk_pool.tile([P, 2, 2 * P], F32)
+            for j in range(2):
+                nc.tensor.matmul_mx(
+                    out=qk[:, j, :],
+                    lhsT=codes[:, P * j : P * (j + 1)].bitcast(FP8X4),
+                    lhsT_scale=planes[:, P * j : P * (j + 1)],
+                    rhs=w_words[:].bitcast(FP4X4),
+                    rhs_scale=w_planes[:],
+                    start=True,
+                    stop=True,
+                )
+            qk_tiles[u] = qk
+
+        def square(u):
+            squares = work.tile([P, 2 * 2 * P], F32)
+            nc.scalar.activation(
+                out=squares[:], in_=qk_tiles[u][:].rearrange("p j e -> p (j e)"), func=ACT.Square
+            )
+            square_tiles[u] = squares
+
+        def sum_squares(u):
+            norms = work.tile([P, GROUPS], F32)
+            nc.vector.tensor_reduce(
+                out=norms[:],
+                in_=square_tiles[u][:].rearrange("p (g d) -> p g d", d=HEAD_DIM),
+                axis=AXIS.X,
+                op=ALU.add,
+            )
+            nc.vector.tensor_scalar_max(out=norms[:], in0=norms[:], scalar1=TINY)
+            norm_tiles[u] = norms
+
+        def root(u):
+            nc.scalar.sqrt(out=norm_tiles[u][:], in_=norm_tiles[u][:])
+
+        def normalise(u):
+            norms = norm_tiles[u]
+            nc.vector.reciprocal(out=norms[:], in_=norms[:])
+            unit = work.tile([P, 4, HEAD_DIM, HEADS], F32)
+            nc.vector.tensor_tensor(
+                out=unit[:],
+                in0=qk_tiles[u][:].rearrange("p j (c h d) -> p (j c) d h", c=2, h=HEADS),
+                in1=norms[:]
+                .rearrange("p (g h) -> p g h", h=HEADS)
+                .unsqueeze(2)
+                .to_broadcast([P, 4, HEAD_DIM, HEADS]),
+                op=ALU.mult,
+            )
+            unit_tiles[u] = unit
+
+        def transpose_out(u):
+            unit = unit_tiles[u]
+            ot = ot_pool.tile([P, 2, 2, P], F32)
+            for c in range(2):
+                for j in range(2):
+                    nc.tensor.transpose(
+                        ot[:, c, j, :], unit[:, 2 * j + c, :, :].rearrange("p d h -> p (d h)"), ident[:]
+                    )
+            ot_tiles[u] = ot
+
+        def store_frame(f):
+            stage = stage_tiles[f]
+            b, t = divmod(f, FRAMES)
+            nc.sync.dma_start(out=q_rows[b, t], in_=stage[:, 0, :])
+            if t > 0:
+                nc.sync.dma_start(out=k_rows[b, t - 1], in_=stage[:, 1, :])
+            if t == FRAMES - 1:
+                nc.sync.dma_start(out=k_rows[b, t], in_=stage[:, 1, :])
+
+        def collect(u):
+            ot = ot_tiles[u]
+            for f in range(PAIR_TOKENS * u // FRAME_TOKENS, (PAIR_TOKENS * (u + 1) - 1) // FRAME_TOKENS + 1):
+                first = max(PAIR_TOKENS * u, FRAME_TOKENS * f)
+                last = min(PAIR_TOKENS * (u + 1), FRAME_TOKENS * (f + 1))
+                if f not in stage_tiles:
+                    stage = stage_pool.tile([P, 2, FRAME_TOKENS], F32)
+                    stage_tiles[f] = stage
+                nc.scalar.copy(
+                    out=stage_tiles[f][
+                        :, :, first - FRAME_TOKENS * f : last - FRAME_TOKENS * f
+                    ].rearrange("e c (n j) -> e c n j", j=2),
+                    in_=ot[
+                        :, :, :, (first - PAIR_TOKENS * u) // 2 : (last - PAIR_TOKENS * u) // 2
+                    ].rearrange("e c j n -> e c n j"),
+                )
+                if last == FRAME_TOKENS * (f + 1):
+                    store_frame(f)
+
+        def live(u):
+            return 0 <= u < PAIRS
+
+        for s in range(PAIRS + LAST_LAG):
+            if live(s - 4):
+                transpose_out(s - 4)
+            if live(s):
+                transpose_x(s)
+            if live(s - 1):
+                quantise_x(s - 1)
+                project(s - 1)
+            if live(s - 3):
+                root(s - 3)
+            if live(s - 2):
+                square(s - 2)
+            if live(s - 4):
+                collect(s - 4)
+            if live(s):
+                group_x(s)
+            if live(s - 3):
+                normalise(s - 3)
+            if live(s - 2):
+                sum_squares(s - 2)
+            if live(s + LOADS_AHEAD):
+                load(s + LOADS_AHEAD)

@@ -24,11 +24,11 @@ HEAD_DIM = 16
 TOKENS = CLIPS * FRAMES * FRAME_TOKENS
 PAIR_TOKENS = 2 * P
 PAIRS = TOKENS // PAIR_TOKENS
-GROUPS = 2 * 2 * HEADS
 TINY = 1e-24
 
 LOADS_AHEAD = 8
-LAST_LAG = 4
+VECTOR_TAKES_EVERY = 4
+LAST_LAG = 6
 
 FLOPS = 2 * TOKENS * CHANNELS * 2 * HEADS * HEAD_DIM
 
@@ -44,11 +44,11 @@ def tile_costvolumeattention17_pa_t_kernel(
     with ExitStack() as ctx:
         const = ctx.enter_context(tc.tile_pool(name="const", bufs=1))
         x_pool = ctx.enter_context(tc.tile_pool(name="x", bufs=LOADS_AHEAD + 1))
-        work = ctx.enter_context(tc.tile_pool(name="work", bufs=3))
+        work = ctx.enter_context(tc.tile_pool(name="work", bufs=4))
         stage_pool = ctx.enter_context(tc.tile_pool(name="stage", bufs=4))
         xt_pool = ctx.enter_context(tc.psum_pool(name="xt", bufs=2))
-        qk_pool = ctx.enter_context(tc.psum_pool(name="qk", bufs=3))
-        ot_pool = ctx.enter_context(tc.psum_pool(name="ot", bufs=3))
+        qk_pool = ctx.enter_context(tc.psum_pool(name="qk", bufs=4))
+        ot_pool = ctx.enter_context(tc.psum_pool(name="ot", bufs=2))
         ctx.enter_context(tc.manual_schedule())
 
         x_tiles = {}
@@ -63,12 +63,17 @@ def tile_costvolumeattention17_pa_t_kernel(
         ot_tiles = {}
         stage_tiles = {}
 
+        def kinds_of(u):
+            first_frame = PAIR_TOKENS * u // FRAME_TOKENS
+            last_frame = (PAIR_TOKENS * (u + 1) - 1) // FRAME_TOKENS
+            return 1 if first_frame == last_frame and first_frame % FRAMES == 0 else 2
+
         def load(u):
             x_sb = x_pool.tile([P, 2 * CHANNELS], BF16)
             nc.sync.dma_start(out=x_sb[:], in_=x_pairs[u])
             x_tiles[u] = x_sb
 
-        load(0)
+        load(PAIRS - 1)
         w_words = const.tile([P, 2 * 2 * P], U8, align_bytes=64)
         w_planes = const.tile([P, 2 * P], U8, align_bytes=64)
         nc.vector.memset(w_planes[:].bitcast(I32), 0)
@@ -81,13 +86,13 @@ def tile_costvolumeattention17_pa_t_kernel(
                     out=w_planes[32 * quad : 32 * quad + 4, P * c : P * (c + 1)].bitcast(I32),
                     in_=scales[0, 4 * quad : 4 * quad + 4, :].bitcast(I32),
                 )
-        for u in range(1, LOADS_AHEAD):
-            load(u)
+        for place in range(1, LOADS_AHEAD):
+            load(PAIRS - 1 - place)
         ident = const.tile([P, P], F32)
         make_identity(nc, ident[:])
         warm = const.tile([P, 1], F32)
         nc.vector.memset(warm[:], 1.0)
-        nc.scalar.sqrt(out=warm[:], in_=warm[:])
+        nc.scalar.activation(out=warm[:], in_=warm[:], func=ACT.Abs_reciprocal_sqrt)
 
         def transpose_x(u):
             words = x_tiles[u][:].bitcast(F32)
@@ -125,62 +130,70 @@ def tile_costvolumeattention17_pa_t_kernel(
         def project(u):
             codes = code_tiles[u]
             planes = plane_tiles[u]
-            qk = qk_pool.tile([P, 2, 2 * P], F32)
+            kinds = kinds_of(u)
+            qk = qk_pool.tile([P, 2, kinds * P], F32)
             for j in range(2):
                 nc.tensor.matmul_mx(
                     out=qk[:, j, :],
                     lhsT=codes[:, P * j : P * (j + 1)].bitcast(FP8X4),
                     lhsT_scale=planes[:, P * j : P * (j + 1)],
-                    rhs=w_words[:].bitcast(FP4X4),
-                    rhs_scale=w_planes[:],
+                    rhs=w_words[:, 0 : 2 * P * kinds].bitcast(FP4X4),
+                    rhs_scale=w_planes[:, 0 : P * kinds],
                     start=True,
                     stop=True,
                 )
             qk_tiles[u] = qk
 
         def square(u):
-            squares = work.tile([P, 2 * 2 * P], F32)
+            squares = work.tile([P, 2 * kinds_of(u) * P], F32)
             nc.scalar.activation(
                 out=squares[:], in_=qk_tiles[u][:].rearrange("p j e -> p (j e)"), func=ACT.Square
             )
             square_tiles[u] = squares
 
         def sum_squares(u):
-            norms = work.tile([P, GROUPS], F32)
+            norms = work.tile([P, 2 * kinds_of(u) * HEADS], F32)
             nc.vector.tensor_reduce(
                 out=norms[:],
                 in_=square_tiles[u][:].rearrange("p (g d) -> p g d", d=HEAD_DIM),
                 axis=AXIS.X,
                 op=ALU.add,
             )
-            nc.vector.tensor_scalar_max(out=norms[:], in0=norms[:], scalar1=TINY)
             norm_tiles[u] = norms
 
-        def root(u):
-            nc.scalar.sqrt(out=norm_tiles[u][:], in_=norm_tiles[u][:])
+        def clamp(u):
+            nc.vector.tensor_scalar_max(out=norm_tiles[u][:], in0=norm_tiles[u][:], scalar1=TINY)
+
+        def inverse_root(u):
+            nc.scalar.activation(
+                out=norm_tiles[u][:], in_=norm_tiles[u][:], func=ACT.Abs_reciprocal_sqrt
+            )
 
         def normalise(u):
             norms = norm_tiles[u]
-            nc.vector.reciprocal(out=norms[:], in_=norms[:])
-            unit = work.tile([P, 4, HEAD_DIM, HEADS], F32)
+            kinds = kinds_of(u)
+            unit = work.tile([P, 2 * kinds, HEAD_DIM, HEADS], F32)
             nc.vector.tensor_tensor(
                 out=unit[:],
-                in0=qk_tiles[u][:].rearrange("p j (c h d) -> p (j c) d h", c=2, h=HEADS),
+                in0=qk_tiles[u][:].rearrange("p j (c h d) -> p (j c) d h", c=kinds, h=HEADS),
                 in1=norms[:]
                 .rearrange("p (g h) -> p g h", h=HEADS)
                 .unsqueeze(2)
-                .to_broadcast([P, 4, HEAD_DIM, HEADS]),
+                .to_broadcast([P, 2 * kinds, HEAD_DIM, HEADS]),
                 op=ALU.mult,
             )
             unit_tiles[u] = unit
 
         def transpose_out(u):
             unit = unit_tiles[u]
-            ot = ot_pool.tile([P, 2, 2, P], F32)
-            for c in range(2):
+            kinds = kinds_of(u)
+            ot = ot_pool.tile([P, kinds, 2, P], F32)
+            for c in range(kinds):
                 for j in range(2):
                     nc.tensor.transpose(
-                        ot[:, c, j, :], unit[:, 2 * j + c, :, :].rearrange("p d h -> p (d h)"), ident[:]
+                        ot[:, c, j, :],
+                        unit[:, kinds * j + c, :, :].rearrange("p d h -> p (d h)"),
+                        ident[:],
                     )
             ot_tiles[u] = ot
 
@@ -195,45 +208,41 @@ def tile_costvolumeattention17_pa_t_kernel(
 
         def collect(u):
             ot = ot_tiles[u]
-            for f in range(PAIR_TOKENS * u // FRAME_TOKENS, (PAIR_TOKENS * (u + 1) - 1) // FRAME_TOKENS + 1):
+            copy_out = nc.vector.tensor_copy if u % VECTOR_TAKES_EVERY == 0 else nc.scalar.copy
+            for f in reversed(
+                range(PAIR_TOKENS * u // FRAME_TOKENS, (PAIR_TOKENS * (u + 1) - 1) // FRAME_TOKENS + 1)
+            ):
                 first = max(PAIR_TOKENS * u, FRAME_TOKENS * f)
                 last = min(PAIR_TOKENS * (u + 1), FRAME_TOKENS * (f + 1))
+                kept = 1 if f % FRAMES == 0 else 2
                 if f not in stage_tiles:
                     stage = stage_pool.tile([P, 2, FRAME_TOKENS], F32)
                     stage_tiles[f] = stage
-                nc.scalar.copy(
+                copy_out(
                     out=stage_tiles[f][
-                        :, :, first - FRAME_TOKENS * f : last - FRAME_TOKENS * f
+                        :, 0:kept, first - FRAME_TOKENS * f : last - FRAME_TOKENS * f
                     ].rearrange("e c (n j) -> e c n j", j=2),
                     in_=ot[
-                        :, :, :, (first - PAIR_TOKENS * u) // 2 : (last - PAIR_TOKENS * u) // 2
+                        :, 0:kept, :, (first - PAIR_TOKENS * u) // 2 : (last - PAIR_TOKENS * u) // 2
                     ].rearrange("e c j n -> e c n j"),
                 )
-                if last == FRAME_TOKENS * (f + 1):
+                if first == FRAME_TOKENS * f:
                     store_frame(f)
 
-        def live(u):
-            return 0 <= u < PAIRS
+        def run(stage, place):
+            if 0 <= place < PAIRS:
+                stage(PAIRS - 1 - place)
 
         for s in range(PAIRS + LAST_LAG):
-            if live(s - 4):
-                transpose_out(s - 4)
-            if live(s):
-                transpose_x(s)
-            if live(s - 1):
-                quantise_x(s - 1)
-                project(s - 1)
-            if live(s - 3):
-                root(s - 3)
-            if live(s - 2):
-                square(s - 2)
-            if live(s - 4):
-                collect(s - 4)
-            if live(s):
-                group_x(s)
-            if live(s - 3):
-                normalise(s - 3)
-            if live(s - 2):
-                sum_squares(s - 2)
-            if live(s + LOADS_AHEAD):
-                load(s + LOADS_AHEAD)
+            run(transpose_out, s - 6)
+            run(transpose_x, s)
+            run(quantise_x, s - 2)
+            run(project, s - 2)
+            run(square, s - 3)
+            run(group_x, s - 1)
+            run(clamp, s - 4)
+            run(inverse_root, s - 4)
+            run(normalise, s - 5)
+            run(collect, s - 6)
+            run(sum_squares, s - 3)
+            run(load, s + LOADS_AHEAD)

@@ -27,8 +27,8 @@ PAIRS = TOKENS // PAIR_TOKENS
 TINY = 1e-24
 
 LOADS_AHEAD = 8
-VECTOR_TAKES_EVERY = 4
-LAST_LAG = 6
+VECTOR_TAKES_EVERY = 2
+LAST_LAG = 8
 
 FLOPS = 2 * TOKENS * CHANNELS * 2 * HEADS * HEAD_DIM
 
@@ -44,7 +44,7 @@ def tile_costvolumeattention17_pa_t_kernel(
     with ExitStack() as ctx:
         const = ctx.enter_context(tc.tile_pool(name="const", bufs=1))
         x_pool = ctx.enter_context(tc.tile_pool(name="x", bufs=LOADS_AHEAD + 1))
-        work = ctx.enter_context(tc.tile_pool(name="work", bufs=4))
+        work = ctx.enter_context(tc.tile_pool(name="work", bufs=5))
         stage_pool = ctx.enter_context(tc.tile_pool(name="stage", bufs=4))
         xt_pool = ctx.enter_context(tc.psum_pool(name="xt", bufs=2))
         qk_pool = ctx.enter_context(tc.psum_pool(name="qk", bufs=4))
@@ -58,6 +58,7 @@ def tile_costvolumeattention17_pa_t_kernel(
         plane_tiles = {}
         qk_tiles = {}
         square_tiles = {}
+        folded_tiles = {}
         norm_tiles = {}
         unit_tiles = {}
         ot_tiles = {}
@@ -151,14 +152,20 @@ def tile_costvolumeattention17_pa_t_kernel(
             )
             square_tiles[u] = squares
 
-        def sum_squares(u):
-            norms = work.tile([P, 2 * kinds_of(u) * HEADS], F32)
-            nc.vector.tensor_reduce(
-                out=norms[:],
-                in_=square_tiles[u][:].rearrange("p (g d) -> p g d", d=HEAD_DIM),
-                axis=AXIS.X,
+        def fold_squares(u):
+            by_head = square_tiles[u][:].rearrange("p (g d) -> p g d", d=HEAD_DIM)
+            folded = work.tile([P, 2 * kinds_of(u) * HEADS, HEAD_DIM // 2], F32)
+            nc.gpsimd.tensor_tensor(
+                out=folded[:],
+                in0=by_head[:, :, 0 : HEAD_DIM // 2],
+                in1=by_head[:, :, HEAD_DIM // 2 : HEAD_DIM],
                 op=ALU.add,
             )
+            folded_tiles[u] = folded
+
+        def sum_squares(u):
+            norms = work.tile([P, 2 * kinds_of(u) * HEADS], F32)
+            nc.vector.tensor_reduce(out=norms[:], in_=folded_tiles[u][:], axis=AXIS.X, op=ALU.add)
             norm_tiles[u] = norms
 
         def clamp(u):
@@ -234,15 +241,16 @@ def tile_costvolumeattention17_pa_t_kernel(
                 stage(PAIRS - 1 - place)
 
         for s in range(PAIRS + LAST_LAG):
-            run(transpose_out, s - 6)
+            run(normalise, s - 7)
+            run(transpose_out, s - 8)
             run(transpose_x, s)
-            run(quantise_x, s - 2)
-            run(project, s - 2)
-            run(square, s - 3)
+            run(project, s - 3)
+            run(square, s - 4)
+            run(fold_squares, s - 4)
+            run(inverse_root, s - 6)
             run(group_x, s - 1)
-            run(clamp, s - 4)
-            run(inverse_root, s - 4)
-            run(normalise, s - 5)
-            run(collect, s - 6)
-            run(sum_squares, s - 3)
+            run(sum_squares, s - 5)
+            run(quantise_x, s - 2)
+            run(clamp, s - 5)
+            run(collect, s - 8)
             run(load, s + LOADS_AHEAD)

@@ -28,7 +28,7 @@ TINY = 1e-24
 
 LOADS_AHEAD = 8
 VECTOR_TAKES_EVERY = 2
-LAST_LAG = 8
+LAST_LAG = 7
 
 FLOPS = 2 * TOKENS * CHANNELS * 2 * HEADS * HEAD_DIM
 
@@ -241,16 +241,16 @@ def tile_costvolumeattention17_pa_t_kernel(
                 stage(PAIRS - 1 - place)
 
         for s in range(PAIRS + LAST_LAG):
-            run(normalise, s - 7)
-            run(transpose_out, s - 8)
-            run(transpose_x, s)
-            run(project, s - 3)
-            run(square, s - 4)
-            run(fold_squares, s - 4)
-            run(inverse_root, s - 6)
-            run(group_x, s - 1)
-            run(sum_squares, s - 5)
-            run(quantise_x, s - 2)
+            run(normalise, s - 6)
             run(clamp, s - 5)
-            run(collect, s - 8)
+            run(transpose_out, s - 7)
+            run(transpose_x, s)
+            run(group_x, s - 1)
+            run(quantise_x, s - 2)
+            run(project, s - 2)
+            run(square, s - 3)
+            run(fold_squares, s - 3)
+            run(inverse_root, s - 5)
+            run(sum_squares, s - 4)
+            run(collect, s - 7)
             run(load, s + LOADS_AHEAD)

@@ -27,6 +27,7 @@ PAIRS = TOKENS // PAIR_TOKENS
 TINY = 1e-24
 
 LOADS_AHEAD = 8
+LOADS_BEFORE_WEIGHTS = 3
 VECTOR_TAKES_EVERY = 2
 LAST_LAG = 7
 
@@ -74,7 +75,8 @@ def tile_costvolumeattention17_pa_t_kernel(
             nc.sync.dma_start(out=x_sb[:], in_=x_pairs[u])
             x_tiles[u] = x_sb
 
-        load(PAIRS - 1)
+        for place in range(LOADS_BEFORE_WEIGHTS):
+            load(PAIRS - 1 - place)
         w_words = const.tile([P, 2 * 2 * P], U8, align_bytes=64)
         w_planes = const.tile([P, 2 * P], U8, align_bytes=64)
         nc.vector.memset(w_planes[:].bitcast(I32), 0)
@@ -87,7 +89,7 @@ def tile_costvolumeattention17_pa_t_kernel(
                     out=w_planes[32 * quad : 32 * quad + 4, P * c : P * (c + 1)].bitcast(I32),
                     in_=scales[0, 4 * quad : 4 * quad + 4, :].bitcast(I32),
                 )
-        for place in range(1, LOADS_AHEAD):
+        for place in range(LOADS_BEFORE_WEIGHTS, LOADS_AHEAD):
             load(PAIRS - 1 - place)
         ident = const.tile([P, P], F32)
         make_identity(nc, ident[:])
@@ -182,11 +184,11 @@ def tile_costvolumeattention17_pa_t_kernel(
             unit = work.tile([P, 2 * kinds, HEAD_DIM, HEADS], F32)
             nc.vector.tensor_tensor(
                 out=unit[:],
-                in0=qk_tiles[u][:].rearrange("p j (c h d) -> p (j c) d h", c=kinds, h=HEADS),
-                in1=norms[:]
+                in0=norms[:]
                 .rearrange("p (g h) -> p g h", h=HEADS)
                 .unsqueeze(2)
                 .to_broadcast([P, 2 * kinds, HEAD_DIM, HEADS]),
+                in1=qk_tiles[u][:].rearrange("p j (c h d) -> p (j c) d h", c=kinds, h=HEADS),
                 op=ALU.mult,
             )
             unit_tiles[u] = unit
@@ -204,14 +206,15 @@ def tile_costvolumeattention17_pa_t_kernel(
                     )
             ot_tiles[u] = ot
 
-        def store_frame(f):
+        def store_frame(f, first, last):
             stage = stage_tiles[f]
             b, t = divmod(f, FRAMES)
-            nc.sync.dma_start(out=q_rows[b, t], in_=stage[:, 0, :])
+            cols = slice(first, last)
+            nc.sync.dma_start(out=q_rows[b, t, :, :, cols], in_=stage[:, 0, cols])
             if t > 0:
-                nc.sync.dma_start(out=k_rows[b, t - 1], in_=stage[:, 1, :])
+                nc.sync.dma_start(out=k_rows[b, t - 1, :, :, cols], in_=stage[:, 1, cols])
             if t == FRAMES - 1:
-                nc.sync.dma_start(out=k_rows[b, t], in_=stage[:, 1, :])
+                nc.sync.dma_start(out=k_rows[b, t, :, :, cols], in_=stage[:, 1, cols])
 
         def collect(u):
             ot = ot_tiles[u]
@@ -233,8 +236,10 @@ def tile_costvolumeattention17_pa_t_kernel(
                         :, 0:kept, :, (first - PAIR_TOKENS * u) // 2 : (last - PAIR_TOKENS * u) // 2
                     ].rearrange("e c j n -> e c n j"),
                 )
-                if first == FRAME_TOKENS * f:
-                    store_frame(f)
+                if f == 0:
+                    store_frame(f, first, last)
+                elif first == FRAME_TOKENS * f:
+                    store_frame(f, 0, FRAME_TOKENS)
 
         def run(stage, place):
             if 0 <= place < PAIRS:

@@ -93,6 +93,10 @@ def tile_costvolumeattention17_pa_t_kernel(
             load(PAIRS - 1 - place)
         ident = const.tile([P, P], F32)
         make_identity(nc, ident[:])
+        below = const.tile([P, 1], F32)
+        nc.vector.memset(below[:], -TINY)
+        above = const.tile([P, 1], F32)
+        nc.vector.memset(above[:], TINY)
         warm = const.tile([P, 1], F32)
         nc.vector.memset(warm[:], 1.0)
         nc.scalar.activation(out=warm[:], in_=warm[:], func=ACT.Abs_reciprocal_sqrt)
@@ -171,11 +175,16 @@ def tile_costvolumeattention17_pa_t_kernel(
             norm_tiles[u] = norms
 
         def clamp(u):
-            nc.vector.tensor_scalar_max(out=norm_tiles[u][:], in0=norm_tiles[u][:], scalar1=TINY)
+            nc.scalar.activation(
+                out=norm_tiles[u][:], in_=norm_tiles[u][:], func=ACT.Relu, bias=below[:]
+            )
 
         def inverse_root(u):
             nc.scalar.activation(
-                out=norm_tiles[u][:], in_=norm_tiles[u][:], func=ACT.Abs_reciprocal_sqrt
+                out=norm_tiles[u][:],
+                in_=norm_tiles[u][:],
+                func=ACT.Abs_reciprocal_sqrt,
+                bias=above[:],
             )
 
         def normalise(u):

@@ -29,7 +29,7 @@ TINY = 1e-24
 LOADS_AHEAD = 8
 LOADS_BEFORE_WEIGHTS = 3
 VECTOR_TAKES_EVERY = 2
-LAST_LAG = 7
+LAST_LAG = 8
 
 FLOPS = 2 * TOKENS * CHANNELS * 2 * HEADS * HEAD_DIM
 
@@ -255,16 +255,16 @@ def tile_costvolumeattention17_pa_t_kernel(
                 stage(PAIRS - 1 - place)
 
         for s in range(PAIRS + LAST_LAG):
-            run(normalise, s - 6)
-            run(clamp, s - 5)
-            run(transpose_out, s - 7)
-            run(transpose_x, s)
-            run(group_x, s - 1)
+            run(normalise, s - 7)
             run(quantise_x, s - 2)
-            run(project, s - 2)
-            run(square, s - 3)
-            run(fold_squares, s - 3)
-            run(inverse_root, s - 5)
-            run(sum_squares, s - 4)
-            run(collect, s - 7)
+            run(clamp, s - 6)
+            run(square, s - 4)
+            run(inverse_root, s - 6)
+            run(group_x, s - 1)
+            run(fold_squares, s - 5)
+            run(sum_squares, s - 5)
+            run(project, s - 3)
+            run(transpose_x, s)
+            run(transpose_out, s - 7)
+            run(collect, s - 8)
             run(load, s + LOADS_AHEAD)

@@ -27,7 +27,6 @@ PAIRS = TOKENS // PAIR_TOKENS
 TINY = 1e-24
 
 LOADS_AHEAD = 8
-LOADS_BEFORE_WEIGHTS = 3
 VECTOR_TAKES_EVERY = 2
 LAST_LAG = 8
 
@@ -75,8 +74,7 @@ def tile_costvolumeattention17_pa_t_kernel(
             nc.sync.dma_start(out=x_sb[:], in_=x_pairs[u])
             x_tiles[u] = x_sb
 
-        for place in range(LOADS_BEFORE_WEIGHTS):
-            load(PAIRS - 1 - place)
+        load(PAIRS - 1)
         w_words = const.tile([P, 2 * 2 * P], U8, align_bytes=64)
         w_planes = const.tile([P, 2 * P], U8, align_bytes=64)
         nc.vector.memset(w_planes[:].bitcast(I32), 0)
@@ -89,7 +87,10 @@ def tile_costvolumeattention17_pa_t_kernel(
                     out=w_planes[32 * quad : 32 * quad + 4, P * c : P * (c + 1)].bitcast(I32),
                     in_=scales[0, 4 * quad : 4 * quad + 4, :].bitcast(I32),
                 )
-        for place in range(LOADS_BEFORE_WEIGHTS, LOADS_AHEAD):
+            if c == 0:
+                load(PAIRS - 2)
+                load(PAIRS - 3)
+        for place in range(3, LOADS_AHEAD):
             load(PAIRS - 1 - place)
         ident = const.tile([P, P], F32)
         make_identity(nc, ident[:])
@@ -152,19 +153,22 @@ def tile_costvolumeattention17_pa_t_kernel(
             qk_tiles[u] = qk
 
         def square(u):
-            squares = work.tile([P, 2 * kinds_of(u) * P], F32)
+            squares = work.tile([P, 2, 2 * kinds_of(u) * HEADS, HEAD_DIM // 2], F32)
             nc.scalar.activation(
-                out=squares[:], in_=qk_tiles[u][:].rearrange("p j e -> p (j e)"), func=ACT.Square
+                out=squares[:],
+                in_=qk_tiles[u][:].rearrange("p j (g half d) -> p half (j g) d", half=2, d=HEAD_DIM // 2),
+                func=ACT.Square,
+                bias=0.0,
             )
             square_tiles[u] = squares
 
         def fold_squares(u):
-            by_head = square_tiles[u][:].rearrange("p (g d) -> p g d", d=HEAD_DIM)
+            squares = square_tiles[u]
             folded = work.tile([P, 2 * kinds_of(u) * HEADS, HEAD_DIM // 2], F32)
             nc.gpsimd.tensor_tensor(
                 out=folded[:],
-                in0=by_head[:, :, 0 : HEAD_DIM // 2],
-                in1=by_head[:, :, HEAD_DIM // 2 : HEAD_DIM],
+                in0=squares[:, 0, :, :],
+                in1=squares[:, 1, :, :],
                 op=ALU.add,
             )
             folded_tiles[u] = folded

@@ -45,7 +45,7 @@ def tile_costvolumeattention17_pa_t_kernel(
         const = ctx.enter_context(tc.tile_pool(name="const", bufs=1))
         x_pool = ctx.enter_context(tc.tile_pool(name="x", bufs=LOADS_AHEAD + 1))
         work = ctx.enter_context(tc.tile_pool(name="work", bufs=5))
-        stage_pool = ctx.enter_context(tc.tile_pool(name="stage", bufs=4))
+        stage_pool = ctx.enter_context(tc.tile_pool(name="stage", bufs=CLIPS * FRAMES))
         xt_pool = ctx.enter_context(tc.psum_pool(name="xt", bufs=2))
         qk_pool = ctx.enter_context(tc.psum_pool(name="qk", bufs=4))
         ot_pool = ctx.enter_context(tc.psum_pool(name="ot", bufs=2))
@@ -74,7 +74,10 @@ def tile_costvolumeattention17_pa_t_kernel(
             nc.sync.dma_start(out=x_sb[:], in_=x_pairs[u])
             x_tiles[u] = x_sb
 
-        load(PAIRS - 1)
+        light = [u for u in reversed(range(PAIRS)) if kinds_of(u) == 1]
+        order = [u for u in reversed(range(PAIRS)) if u not in light] + light
+
+        load(order[0])
         w_words = const.tile([P, 2 * 2 * P], U8, align_bytes=64)
         w_planes = const.tile([P, 2 * P], U8, align_bytes=64)
         nc.vector.memset(w_planes[:].bitcast(I32), 0)
@@ -88,10 +91,10 @@ def tile_costvolumeattention17_pa_t_kernel(
                     in_=scales[0, 4 * quad : 4 * quad + 4, :].bitcast(I32),
                 )
             if c == 0:
-                load(PAIRS - 2)
-                load(PAIRS - 3)
+                load(order[1])
+                load(order[2])
         for place in range(3, LOADS_AHEAD):
-            load(PAIRS - 1 - place)
+            load(order[place])
         ident = const.tile([P, P], F32)
         make_identity(nc, ident[:])
         below = const.tile([P, 1], F32)
@@ -249,14 +252,14 @@ def tile_costvolumeattention17_pa_t_kernel(
                         :, 0:kept, :, (first - PAIR_TOKENS * u) // 2 : (last - PAIR_TOKENS * u) // 2
                     ].rearrange("e c j n -> e c n j"),
                 )
-                if f == 0:
-                    store_frame(f, first, last)
+                if f % FRAMES == 0:
+                    store_frame(f, first - FRAME_TOKENS * f, last - FRAME_TOKENS * f)
                 elif first == FRAME_TOKENS * f:
                     store_frame(f, 0, FRAME_TOKENS)
 
         def run(stage, place):
             if 0 <= place < PAIRS:
-                stage(PAIRS - 1 - place)
+                stage(order[place])
 
         for s in range(PAIRS + LAST_LAG):
             run(normalise, s - 7)

@@ -18,12 +18,15 @@ P = 128
 CLIPS = 2
 FRAMES = 8
 FRAME_TOKENS = 28 * 28
+CLIP_TOKENS = FRAMES * FRAME_TOKENS
 CHANNELS = 512
 HEADS = 8
 HEAD_DIM = 16
-TOKENS = CLIPS * FRAMES * FRAME_TOKENS
+TOKENS = CLIPS * CLIP_TOKENS
 PAIR_TOKENS = 2 * P
-PAIRS = TOKENS // PAIR_TOKENS
+CLIP_PAIRS = CLIP_TOKENS // PAIR_TOKENS
+PAIRS = CLIPS * CLIP_PAIRS + 1
+MIXED = CLIPS * CLIP_PAIRS
 TINY = 1e-24
 
 LOADS_AHEAD = 8
@@ -37,7 +40,6 @@ def tile_costvolumeattention17_pa_t_kernel(
     tc, x, q_w_words, q_w_scales, k_w_words, k_w_scales, out_0, out_1
 ):
     nc = tc.nc
-    x_pairs = x.rearrange("b n c -> (b n) c").rearrange("(u p j) c -> u p (j c)", p=P, j=2)
     q_rows = out_0.rearrange("(b h t) d i j -> b t d h (i j)", b=CLIPS, h=HEADS)
     k_rows = out_1.rearrange("(b h t) d i j -> b t d h (i j)", b=CLIPS, h=HEADS)
 
@@ -65,13 +67,25 @@ def tile_costvolumeattention17_pa_t_kernel(
         stage_tiles = {}
 
         def kinds_of(u):
-            first_frame = PAIR_TOKENS * u // FRAME_TOKENS
-            last_frame = (PAIR_TOKENS * (u + 1) - 1) // FRAME_TOKENS
-            return 1 if first_frame == last_frame and first_frame % FRAMES == 0 else 2
+            i = u % CLIP_PAIRS
+            return 1 if u != MIXED and PAIR_TOKENS * (i + 1) <= FRAME_TOKENS else 2
 
         def load(u):
             x_sb = x_pool.tile([P, 2 * CHANNELS], BF16)
-            nc.sync.dma_start(out=x_sb[:], in_=x_pairs[u])
+            if u == MIXED:
+                for j in range(CLIPS):
+                    nc.sync.dma_start(
+                        out=x_sb[:, CHANNELS * j : CHANNELS * (j + 1)],
+                        in_=x[j, PAIR_TOKENS * CLIP_PAIRS : CLIP_TOKENS, :],
+                    )
+            else:
+                b, i = divmod(u, CLIP_PAIRS)
+                nc.sync.dma_start(
+                    out=x_sb[:],
+                    in_=x[b, PAIR_TOKENS * i : PAIR_TOKENS * (i + 1), :].rearrange(
+                        "(p j) c -> p (j c)", j=2
+                    ),
+                )
             x_tiles[u] = x_sb
 
         light = [u for u in reversed(range(PAIRS)) if kinds_of(u) == 1]
@@ -232,29 +246,39 @@ def tile_costvolumeattention17_pa_t_kernel(
             if t == FRAMES - 1:
                 nc.sync.dma_start(out=k_rows[b, t, :, :, cols], in_=stage[:, 1, cols])
 
+        def stage_of(f):
+            if f not in stage_tiles:
+                stage = stage_pool.tile([P, 2, FRAME_TOKENS], F32)
+                stage_tiles[f] = stage
+            return stage_tiles[f]
+
         def collect(u):
             ot = ot_tiles[u]
+            if u == MIXED:
+                for j, copy_out in enumerate((nc.vector.tensor_copy, nc.scalar.copy)):
+                    stage = stage_of(FRAMES * j + FRAMES - 1)
+                    copy_out(out=stage[:, :, FRAME_TOKENS - P : FRAME_TOKENS], in_=ot[:, :, j, :])
+                return
             copy_out = nc.vector.tensor_copy if u % VECTOR_TAKES_EVERY == 0 else nc.scalar.copy
-            for f in reversed(
-                range(PAIR_TOKENS * u // FRAME_TOKENS, (PAIR_TOKENS * (u + 1) - 1) // FRAME_TOKENS + 1)
-            ):
-                first = max(PAIR_TOKENS * u, FRAME_TOKENS * f)
-                last = min(PAIR_TOKENS * (u + 1), FRAME_TOKENS * (f + 1))
-                kept = 1 if f % FRAMES == 0 else 2
-                if f not in stage_tiles:
-                    stage = stage_pool.tile([P, 2, FRAME_TOKENS], F32)
-                    stage_tiles[f] = stage
+            b, i = divmod(u, CLIP_PAIRS)
+            start = PAIR_TOKENS * i
+            for t in reversed(range(start // FRAME_TOKENS, (start + PAIR_TOKENS - 1) // FRAME_TOKENS + 1)):
+                first = max(start, FRAME_TOKENS * t)
+                last = min(start + PAIR_TOKENS, FRAME_TOKENS * (t + 1))
+                kept = 1 if t == 0 else 2
+                f = FRAMES * b + t
+                stage = stage_of(f)
                 copy_out(
-                    out=stage_tiles[f][
-                        :, 0:kept, first - FRAME_TOKENS * f : last - FRAME_TOKENS * f
-                    ].rearrange("e c (n j) -> e c n j", j=2),
-                    in_=ot[
-                        :, 0:kept, :, (first - PAIR_TOKENS * u) // 2 : (last - PAIR_TOKENS * u) // 2
-                    ].rearrange("e c j n -> e c n j"),
+                    out=stage[:, 0:kept, first - FRAME_TOKENS * t : last - FRAME_TOKENS * t].rearrange(
+                        "e c (n j) -> e c n j", j=2
+                    ),
+                    in_=ot[:, 0:kept, :, (first - start) // 2 : (last - start) // 2].rearrange(
+                        "e c j n -> e c n j"
+                    ),
                 )
-                if f % FRAMES == 0:
-                    store_frame(f, first - FRAME_TOKENS * f, last - FRAME_TOKENS * f)
-                elif first == FRAME_TOKENS * f:
+                if t == 0:
+                    store_frame(f, first - FRAME_TOKENS * t, last - FRAME_TOKENS * t)
+                elif first == FRAME_TOKENS * t:
                     store_frame(f, 0, FRAME_TOKENS)
 
         def run(stage, place):

@@ -31,6 +31,7 @@ TINY = 1e-24
 
 LOADS_AHEAD = 8
 VECTOR_TAKES_EVERY = 2
+UNFOLDED = 3
 LAST_LAG = 8
 
 FLOPS = 2 * TOKENS * CHANNELS * 2 * HEADS * HEAD_DIM
@@ -90,6 +91,8 @@ def tile_costvolumeattention17_pa_t_kernel(
 
         light = [u for u in reversed(range(PAIRS)) if kinds_of(u) == 1]
         order = [u for u in reversed(range(PAIRS)) if u not in light] + light
+        whole = [u for u in order if u != MIXED]
+        unfolded = order[PAIRS - UNFOLDED :]
 
         load(order[0])
         w_words = const.tile([P, 2 * 2 * P], U8, align_bytes=64)
@@ -180,6 +183,8 @@ def tile_costvolumeattention17_pa_t_kernel(
             square_tiles[u] = squares
 
         def fold_squares(u):
+            if u in unfolded:
+                return
             squares = square_tiles[u]
             folded = work.tile([P, 2 * kinds_of(u) * HEADS, HEAD_DIM // 2], F32)
             nc.gpsimd.tensor_tensor(
@@ -192,7 +197,15 @@ def tile_costvolumeattention17_pa_t_kernel(
 
         def sum_squares(u):
             norms = work.tile([P, 2 * kinds_of(u) * HEADS], F32)
-            nc.vector.tensor_reduce(out=norms[:], in_=folded_tiles[u][:], axis=AXIS.X, op=ALU.add)
+            if u in unfolded:
+                nc.vector.tensor_reduce(
+                    out=norms[:],
+                    in_=square_tiles[u][:].rearrange("p half g d -> p g half d"),
+                    axis=AXIS.XY,
+                    op=ALU.add,
+                )
+            else:
+                nc.vector.tensor_reduce(out=norms[:], in_=folded_tiles[u][:], axis=AXIS.X, op=ALU.add)
             norm_tiles[u] = norms
 
         def clamp(u):
@@ -259,7 +272,8 @@ def tile_costvolumeattention17_pa_t_kernel(
                     stage = stage_of(FRAMES * j + FRAMES - 1)
                     copy_out(out=stage[:, :, FRAME_TOKENS - P : FRAME_TOKENS], in_=ot[:, :, j, :])
                 return
-            copy_out = nc.vector.tensor_copy if u % VECTOR_TAKES_EVERY == 0 else nc.scalar.copy
+            vector_takes = whole.index(u) % VECTOR_TAKES_EVERY == 0
+            copy_out = nc.vector.tensor_copy if vector_takes else nc.scalar.copy
             b, i = divmod(u, CLIP_PAIRS)
             start = PAIR_TOKENS * i
             for t in reversed(range(start // FRAME_TOKENS, (start + PAIR_TOKENS - 1) // FRAME_TOKENS + 1)):

from contextlib import ExitStack

import concourse.mybir as mybir
from concourse.masks import make_identity

F32 = mybir.dt.float32
BF16 = mybir.dt.bfloat16
I32 = mybir.dt.int32
U32 = mybir.dt.uint32
U8 = mybir.dt.uint8
FP8X4 = mybir.dt.float8_e4m3fn_x4
FP4X4 = mybir.dt.float4_e2m1fn_x4
ACT = mybir.ActivationFunctionType
ALU = mybir.AluOpType
AXIS = mybir.AxisListType

P = 128
CLIPS = 2
FRAMES = 8
FRAME_TOKENS = 28 * 28
CLIP_TOKENS = FRAMES * FRAME_TOKENS
CHANNELS = 512
HEADS = 8
HEAD_DIM = 16
TOKENS = CLIPS * CLIP_TOKENS
PAIR_TOKENS = 2 * P
CLIP_PAIRS = CLIP_TOKENS // PAIR_TOKENS
PAIRS = CLIPS * CLIP_PAIRS + 1
MIXED = CLIPS * CLIP_PAIRS
TINY = 1e-24

LOADS_AHEAD = 8
VECTOR_TAKES_EVERY = 2
UNFOLDED = 3
LAST_LAG = 8

FLOPS = 2 * TOKENS * CHANNELS * 2 * HEADS * HEAD_DIM


def tile_costvolumeattention17_pa_t_kernel(
    tc, x, q_w_words, q_w_scales, k_w_words, k_w_scales, out_0, out_1
):
    nc = tc.nc
    q_rows = out_0.rearrange("(b h t) d i j -> b t d h (i j)", b=CLIPS, h=HEADS)
    k_rows = out_1.rearrange("(b h t) d i j -> b t d h (i j)", b=CLIPS, h=HEADS)

    with ExitStack() as ctx:
        const = ctx.enter_context(tc.tile_pool(name="const", bufs=1))
        x_pool = ctx.enter_context(tc.tile_pool(name="x", bufs=LOADS_AHEAD + 1))
        work = ctx.enter_context(tc.tile_pool(name="work", bufs=5))
        stage_pool = ctx.enter_context(tc.tile_pool(name="stage", bufs=CLIPS * FRAMES))
        xt_pool = ctx.enter_context(tc.psum_pool(name="xt", bufs=2))
        qk_pool = ctx.enter_context(tc.psum_pool(name="qk", bufs=4))
        ot_pool = ctx.enter_context(tc.psum_pool(name="ot", bufs=2))
        ctx.enter_context(tc.manual_schedule())

        x_tiles = {}
        xt_tiles = {}
        grouped_tiles = {}
        code_tiles = {}
        plane_tiles = {}
        qk_tiles = {}
        square_tiles = {}
        folded_tiles = {}
        norm_tiles = {}
        unit_tiles = {}
        ot_tiles = {}
        stage_tiles = {}

        def kinds_of(u):
            i = u % CLIP_PAIRS
            return 1 if u != MIXED and PAIR_TOKENS * (i + 1) <= FRAME_TOKENS else 2

        def load(u):
            x_sb = x_pool.tile([P, 2 * CHANNELS], BF16)
            if u == MIXED:
                for j in range(CLIPS):
                    nc.sync.dma_start(
                        out=x_sb[:, CHANNELS * j : CHANNELS * (j + 1)],
                        in_=x[j, PAIR_TOKENS * CLIP_PAIRS : CLIP_TOKENS, :],
                    )
            else:
                b, i = divmod(u, CLIP_PAIRS)
                nc.sync.dma_start(
                    out=x_sb[:],
                    in_=x[b, PAIR_TOKENS * i : PAIR_TOKENS * (i + 1), :].rearrange(
                        "(p j) c -> p (j c)", j=2
                    ),
                )
            x_tiles[u] = x_sb

        light = [u for u in reversed(range(PAIRS)) if kinds_of(u) == 1]
        order = [u for u in reversed(range(PAIRS)) if u not in light] + light
        whole = [u for u in order if u != MIXED]
        unfolded = order[PAIRS - UNFOLDED :]

        load(order[0])
        w_words = const.tile([P, 2 * 2 * P], U8, align_bytes=64)
        w_planes = const.tile([P, 2 * P], U8, align_bytes=64)
        nc.vector.memset(w_planes[:].bitcast(I32), 0)
        for c, (words, scales) in enumerate(((q_w_words, q_w_scales), (k_w_words, k_w_scales))):
            nc.sync.dma_start(
                out=w_words[:, 2 * P * c : 2 * P * (c + 1)].bitcast(I32), in_=words[0].bitcast(I32)
            )
            for quad in range(4):
                nc.sync.dma_start(
                    out=w_planes[32 * quad : 32 * quad + 4, P * c : P * (c + 1)].bitcast(I32),
                    in_=scales[0, 4 * quad : 4 * quad + 4, :].bitcast(I32),
                )
            if c == 0:
                load(order[1])
                load(order[2])
        for place in range(3, LOADS_AHEAD):
            load(order[place])
        ident = const.tile([P, P], F32)
        make_identity(nc, ident[:])
        below = const.tile([P, 1], F32)
        nc.vector.memset(below[:], -TINY)
        above = const.tile([P, 1], F32)
        nc.vector.memset(above[:], TINY)
        warm = const.tile([P, 1], F32)
        nc.vector.memset(warm[:], 1.0)
        nc.scalar.activation(out=warm[:], in_=warm[:], func=ACT.Abs_reciprocal_sqrt)

        def transpose_x(u):
            words = x_tiles[u][:].bitcast(F32)
            xt = xt_pool.tile([P, 2, 2, P], F32)
            for j in range(2):
                for half in range(2):
                    first = (CHANNELS // 2) * j + half
                    nc.tensor.transpose(
                        xt[:, j, half, :], words[:, first : (CHANNELS // 2) * (j + 1) : 2], ident[:]
                    )
            xt_tiles[u] = xt

        def group_x(u):
            grouped = work.tile([P, 2, P, 4], BF16, align_bytes=64)
            nc.scalar.copy(
                out=grouped[:]
                .rearrange("p j n t -> p (j n t)")
                .bitcast(F32)
                .rearrange("p (j n half) -> p j n half", j=2, half=2),
                in_=xt_tiles[u][:].rearrange("p j half n -> p j n half"),
            )
            grouped_tiles[u] = grouped

        def quantise_x(u):
            codes = work.tile([P, PAIR_TOKENS], U32, align_bytes=64)
            planes = work.tile([P, PAIR_TOKENS], U8, align_bytes=64)
            nc.vector.quantize_mx(
                out=codes[:].bitcast(FP8X4),
                scales=planes[:],
                in_=grouped_tiles[u][:].rearrange("p j n t -> p (j n t)"),
            )
            code_tiles[u] = codes
            plane_tiles[u] = planes

        def project(u):
            codes = code_tiles[u]
            planes = plane_tiles[u]
            kinds = kinds_of(u)
            qk = qk_pool.tile([P, 2, kinds * P], F32)
            for j in range(2):
                nc.tensor.matmul_mx(
                    out=qk[:, j, :],
                    lhsT=codes[:, P * j : P * (j + 1)].bitcast(FP8X4),
                    lhsT_scale=planes[:, P * j : P * (j + 1)],
                    rhs=w_words[:, 0 : 2 * P * kinds].bitcast(FP4X4),
                    rhs_scale=w_planes[:, 0 : P * kinds],
                    start=True,
                    stop=True,
                )
            qk_tiles[u] = qk

        def square(u):
            squares = work.tile([P, 2, 2 * kinds_of(u) * HEADS, HEAD_DIM // 2], F32)
            nc.scalar.activation(
                out=squares[:],
                in_=qk_tiles[u][:].rearrange("p j (g half d) -> p half (j g) d", half=2, d=HEAD_DIM // 2),
                func=ACT.Square,
                bias=0.0,
            )
            square_tiles[u] = squares

        def fold_squares(u):
            if u in unfolded:
                return
            squares = square_tiles[u]
            folded = work.tile([P, 2 * kinds_of(u) * HEADS, HEAD_DIM // 2], F32)
            nc.gpsimd.tensor_tensor(
                out=folded[:],
                in0=squares[:, 0, :, :],
                in1=squares[:, 1, :, :],
                op=ALU.add,
            )
            folded_tiles[u] = folded

        def sum_squares(u):
            norms = work.tile([P, 2 * kinds_of(u) * HEADS], F32)
            if u in unfolded:
                nc.vector.tensor_reduce(
                    out=norms[:],
                    in_=square_tiles[u][:].rearrange("p half g d -> p g half d"),
                    axis=AXIS.XY,
                    op=ALU.add,
                )
            else:
                nc.vector.tensor_reduce(out=norms[:], in_=folded_tiles[u][:], axis=AXIS.X, op=ALU.add)
            norm_tiles[u] = norms

        def clamp(u):
            nc.scalar.activation(
                out=norm_tiles[u][:], in_=norm_tiles[u][:], func=ACT.Relu, bias=below[:]
            )

        def inverse_root(u):
            nc.scalar.activation(
                out=norm_tiles[u][:],
                in_=norm_tiles[u][:],
                func=ACT.Abs_reciprocal_sqrt,
                bias=above[:],
            )

        def normalise(u):
            norms = norm_tiles[u]
            kinds = kinds_of(u)
            unit = work.tile([P, 2 * kinds, HEAD_DIM, HEADS], F32)
            nc.vector.tensor_tensor(
                out=unit[:],
                in0=norms[:]
                .rearrange("p (g h) -> p g h", h=HEADS)
                .unsqueeze(2)
                .to_broadcast([P, 2 * kinds, HEAD_DIM, HEADS]),
                in1=qk_tiles[u][:].rearrange("p j (c h d) -> p (j c) d h", c=kinds, h=HEADS),
                op=ALU.mult,
            )
            unit_tiles[u] = unit

        def transpose_out(u):
            unit = unit_tiles[u]
            kinds = kinds_of(u)
            ot = ot_pool.tile([P, kinds, 2, P], F32)
            for c in range(kinds):
                for j in range(2):
                    nc.tensor.transpose(
                        ot[:, c, j, :],
                        unit[:, kinds * j + c, :, :].rearrange("p d h -> p (d h)"),
                        ident[:],
                    )
            ot_tiles[u] = ot

        def store_frame(f, first, last):
            stage = stage_tiles[f]
            b, t = divmod(f, FRAMES)
            cols = slice(first, last)
            nc.sync.dma_start(out=q_rows[b, t, :, :, cols], in_=stage[:, 0, cols])
            if t > 0:
                nc.sync.dma_start(out=k_rows[b, t - 1, :, :, cols], in_=stage[:, 1, cols])
            if t == FRAMES - 1:
                nc.sync.dma_start(out=k_rows[b, t, :, :, cols], in_=stage[:, 1, cols])

        def stage_of(f):
            if f not in stage_tiles:
                stage = stage_pool.tile([P, 2, FRAME_TOKENS], F32)
                stage_tiles[f] = stage
            return stage_tiles[f]

        def collect(u):
            ot = ot_tiles[u]
            if u == MIXED:
                for j, copy_out in enumerate((nc.vector.tensor_copy, nc.scalar.copy)):
                    stage = stage_of(FRAMES * j + FRAMES - 1)
                    copy_out(out=stage[:, :, FRAME_TOKENS - P : FRAME_TOKENS], in_=ot[:, :, j, :])
                return
            vector_takes = whole.index(u) % VECTOR_TAKES_EVERY == 0
            copy_out = nc.vector.tensor_copy if vector_takes else nc.scalar.copy
            b, i = divmod(u, CLIP_PAIRS)
            start = PAIR_TOKENS * i
            for t in reversed(range(start // FRAME_TOKENS, (start + PAIR_TOKENS - 1) // FRAME_TOKENS + 1)):
                first = max(start, FRAME_TOKENS * t)
                last = min(start + PAIR_TOKENS, FRAME_TOKENS * (t + 1))
                kept = 1 if t == 0 else 2
                f = FRAMES * b + t
                stage = stage_of(f)
                copy_out(
                    out=stage[:, 0:kept, first - FRAME_TOKENS * t : last - FRAME_TOKENS * t].rearrange(
                        "e c (n j) -> e c n j", j=2
                    ),
                    in_=ot[:, 0:kept, :, (first - start) // 2 : (last - start) // 2].rearrange(
                        "e c j n -> e c n j"
                    ),
                )
                if t == 0:
                    store_frame(f, first - FRAME_TOKENS * t, last - FRAME_TOKENS * t)
                elif first == FRAME_TOKENS * t:
                    store_frame(f, 0, FRAME_TOKENS)

        def run(stage, place):
            if 0 <= place < PAIRS:
                stage(order[place])

        for s in range(PAIRS + LAST_LAG):
            run(normalise, s - 7)
            run(quantise_x, s - 2)
            run(clamp, s - 6)
            run(square, s - 4)
            run(inverse_root, s - 6)
            run(group_x, s - 1)
            run(fold_squares, s - 5)
            run(sum_squares, s - 5)
            run(project, s - 3)
            run(transpose_x, s)
            run(transpose_out, s - 7)
            run(collect, s - 8)
            run(load, s + LOADS_AHEAD)
